import numpy as np
import ml_dtypes


def mxq(x, axis, fmt="e4m3"):
    dtype, down = {"e4m3": (ml_dtypes.float8_e4m3fn, 7), "e5m2": (ml_dtypes.float8_e5m2, 14)}[fmt]
    v = np.moveaxis(np.asarray(x, np.float32).astype(ml_dtypes.bfloat16).astype(np.float64), axis, -1)
    blocks = v.reshape(v.shape[:-1] + (-1, 32))
    amax = np.abs(blocks).max(-1, keepdims=True)
    byte = np.maximum(np.where(amax > 0, np.frexp(amax)[1] - 1 + 127, 0) - down, 1)
    scale = np.exp2(byte - 127.0)
    codes = (blocks / scale).astype(np.float32).astype(dtype).astype(np.float64)
    return np.moveaxis((codes * scale).reshape(v.shape), -1, axis)


WIDE = False


def mx_kscale(k):
    if not WIDE:
        return np.ones(k)
    levels = np.array([10, -10, 5, -5, 0])
    a = np.random.permutation(np.resize(levels, k // 512 * 4)).reshape(k // 512, 4)
    idx = np.arange(k)
    return np.exp2(a[idx // 512, idx % 128 // 32])


BF16 = ml_dtypes.bfloat16


def bf(x):
    return np.asarray(x, np.float32).astype(BF16)


def f64(x):
    return np.asarray(x).astype(np.float64)


E2M1 = np.array([0.0, 0.5, 1.0, 1.5, 2.0, 3.0, 4.0, 6.0, -0.0, -0.5, -1.0, -1.5, -2.0, -3.0, -4.0, -6.0])


def pack_weight(w, fmt):
    k, n = w.shape
    w = f64(bf(w)).reshape(k // 32, 32, n)
    amax = np.abs(w).max(1)
    if fmt == "e4m3":
        byte = np.frexp(amax)[1] - 1 + 127 - 7
    else:
        mant, ex = np.frexp(amax / 6.0)
        byte = np.where(mant > 0.5, ex, ex - 1) + 127
    byte = np.clip(np.where(amax > 0, byte, 1), 1, 254)
    scaled = (w * np.exp2(127.0 - byte)[:, None, :]).reshape(k, n).astype(np.float32)
    by_word = np.ascontiguousarray(scaled.reshape(k // 512, 128, 4, n).transpose(0, 1, 3, 2))
    if fmt == "e4m3":
        words = by_word.astype(ml_dtypes.float8_e4m3fn).view(np.uint8)
    else:
        c = by_word.astype(ml_dtypes.float4_e2m1fn).view(np.uint8) & 0xF
        words = c[..., 0::2] | (c[..., 1::2] << 4)
    return np.ascontiguousarray(words), np.ascontiguousarray(byte.astype(np.uint8).reshape(k // 512, 16, n))


def unpack_weight(words, scales, fmt):
    g, p, n, _ = words.shape
    if fmt == "e4m3":
        vals = np.ascontiguousarray(words).view(ml_dtypes.float8_e4m3fn).astype(np.float64)
    else:
        nib = np.empty((g, p, n, 4), np.uint8)
        nib[..., 0::2] = words & 0xF
        nib[..., 1::2] = words >> 4
        vals = E2M1[nib]
    vals = vals * np.repeat(np.exp2(scales.astype(np.float64) - 127.0), 8, axis=1)[..., None]
    return vals.transpose(0, 1, 3, 2).reshape(g * 512, n)


B, S, D, H, DH, L, R = 8, 512, 2048, 4, 128, 2048, 64
DV = L - L // 2


def setup_inputs():
    u = mx_kscale(DV)
    q_rot = bf(np.random.standard_normal((B, S, H, DH)))
    k_rot = bf(np.random.standard_normal((B, S, H, DH)))
    c_v = bf(np.random.standard_normal((B, S, DV)) * u)
    words, scales = pack_weight(np.random.standard_normal((DV, H * DH)) * 3.0 / np.sqrt(DV) / u[:, None], "e4m3")
    return {"q_rot": q_rot,
            "k_rot": k_rot,
            "c_v": c_v,
            "W_v_dec_words": words,
            "W_v_dec_scales": scales}


def reference(q_rot, k_rot, c_v, W_v_dec_words, W_v_dec_scales):
    v = (mxq(f64(c_v), 2, "e4m3") @ unpack_weight(W_v_dec_words, W_v_dec_scales, "e4m3")).reshape(B, S, H, DH)
    sc = f64(q_rot).transpose(0, 2, 1, 3) @ f64(k_rot).transpose(0, 2, 3, 1) * (1.0 / np.sqrt(DH))
    e = np.exp(sc - sc.max(-1, keepdims=True))
    ctx = (mxq(e, 3, "e4m3") @ mxq(v.transpose(0, 2, 1, 3), 2, "e4m3")) / e.sum(-1, keepdims=True)
    return ctx.transpose(0, 2, 1, 3).reshape(B, S, H * DH)

@@ -1,0 +1,340 @@
+import math
+from contextlib import ExitStack
+
+import concourse.mybir as mybir
+from concourse.masks import make_identity
+
+F32 = mybir.dt.float32
+BF16 = mybir.dt.bfloat16
+U32 = mybir.dt.uint32
+U8 = mybir.dt.uint8
+I32 = mybir.dt.int32
+FP8X4 = mybir.dt.float8_e4m3fn_x4
+ALU = mybir.AluOpType
+
+B, S, H, DH, DV = 8, 512, 4, 128, 1024
+P = 128
+PACK = 4
+K_PASS = P * PACK
+G = DV // K_PASS
+TILES = S // P
+UNITS = B * H
+SCALE = 1.0 / math.sqrt(DH)
+FLOPS = 2 * B * S * DV * H * DH + 4 * B * H * S * S * DH
+
+
+def tile_multiheadlatentattention_pb_t_kernel(
+    tc, q_rot, k_rot, c_v, W_v_dec_words, W_v_dec_scales, out
+):
+    nc = tc.nc
+    with ExitStack() as ctx:
+        const = ctx.enter_context(tc.tile_pool(name="const", bufs=1))
+        inputs = ctx.enter_context(tc.tile_pool(name="inputs", bufs=3))
+        work = ctx.enter_context(tc.tile_pool(name="work", bufs=2))
+        stats = ctx.enter_context(tc.tile_pool(name="stats", bufs=4))
+        ps_scores = ctx.enter_context(tc.psum_pool(name="ps_scores", bufs=3))
+        ps_eT = ctx.enter_context(tc.psum_pool(name="ps_eT", bufs=2))
+        ps_ctx = ctx.enter_context(tc.psum_pool(name="ps_ctx", bufs=1))
+        ps_prep = ctx.enter_context(tc.psum_pool(name="ps_prep", bufs=2))
+        ctx.enter_context(tc.manual_schedule())
+
+        q_in, k_in, cv_in = {}, {}, {}
+        qk_bank, qkT = {}, {}
+        cv_bank, cv_grouped, cv_codes, cv_scales = {}, {}, {}, {}
+        v_bank, v_grouped, v_codes, v_scales = {}, {}, {}, {}
+        sc, rowmax, bias, rowsum, recip = {}, {}, {}, {}, {}
+        e, eT_bank, e_grouped, e_codes, e_scales = {}, {}, {}, {}, {}
+        ctx_bank = {}
+
+        ident_f32 = const.tile([P, P], F32)
+        make_identity(nc, ident_f32[:])
+        ident_bf16 = const.tile([P, P], BF16)
+        make_identity(nc, ident_bf16[:])
+        w_codes = const.tile([P, G, H * DH], U32, align_bytes=64)
+        w_scales = const.tile([P, G, H * DH], U8, align_bytes=64)
+        nc.vector.memset(w_scales[:].bitcast(I32), 0)
+
+        def load_batch(b):
+            if not 0 <= b < B:
+                return
+            cv_in[b] = inputs.tile([P, TILES, DV], BF16, name="cv_in")
+            for u in range(2):
+                nc.sync.dma_start(
+                    out=cv_in[b][:, 2 * u : 2 * u + 2, :],
+                    in_=c_v[b, 256 * u : 256 * (u + 1), :].rearrange("(p e) k -> p e k", e=2),
+                )
+            q_in[b] = inputs.tile([P, TILES, H * DH], BF16, name="q_in")
+            nc.sync.dma_start(
+                out=q_in[b][:], in_=q_rot[b].rearrange("(p t) h d -> p t (h d)", t=TILES)
+            )
+            k_in[b] = inputs.tile([P, TILES, H * DH], BF16, name="k_in")
+            nc.sync.dma_start(
+                out=k_in[b][:], in_=k_rot[b].rearrange("(t p) h d -> p t (h d)", p=P)
+            )
+
+        def load_weight():
+            for g in range(G):
+                nc.sync.dma_start(
+                    out=w_codes[:, g, :].bitcast(I32),
+                    in_=W_v_dec_words[g].rearrange("p n t -> p (n t)").bitcast(I32),
+                )
+            scale_rows = W_v_dec_scales.bitcast(I32)
+            for quadrant in range(4):
+                nc.sync.dma_start(
+                    out=w_scales[32 * quadrant : 32 * quadrant + 4, :, :].bitcast(I32),
+                    in_=scale_rows[:, 4 * quadrant : 4 * quadrant + 4, :].rearrange(
+                        "g r n -> r g n"
+                    ),
+                )
+
+        def qk_transposes(u):
+            if not 0 <= u + 2 < UNITS:
+                return
+            b, h = divmod(u + 2, H)
+            qk_bank[u] = ps_prep.tile([P, 2, TILES, P], BF16, name="qk_bank", tag="prep")
+            for t in range(TILES):
+                nc.tensor.transpose(
+                    qk_bank[u][:, 0, t, :], q_in[b][:, t, h * DH : (h + 1) * DH], ident_bf16[:]
+                )
+            for t in range(TILES):
+                nc.tensor.transpose(
+                    qk_bank[u][:, 1, t, :], k_in[b][:, t, h * DH : (h + 1) * DH], ident_bf16[:]
+                )
+
+        def qk_copy(u):
+            if not 0 <= u + 2 < UNITS:
+                return
+            qkT[u + 2] = work.tile([P, 2, S], BF16, name="qkT", bufs=4)
+            nc.scalar.copy(
+                out=qkT[u + 2][:], in_=qk_bank[u][:].rearrange("p w t c -> p w (t c)")
+            )
+
+        def latent_part(u):
+            b, part = divmod(u + H, H)
+            pair, g = divmod(part, G)
+            return b, pair, g
+
+        def latent_transposes(u):
+            b, pair, g = latent_part(u)
+            if not 0 <= b < B:
+                return
+            cv_bank[u] = ps_prep.tile([P, 2, 2 * P], F32, name="cv_bank", tag="prep")
+            for j in range(2):
+                words = cv_in[b][:, 2 * pair + j, :].bitcast(F32)
+                for w in range(2):
+                    nc.tensor.transpose(
+                        cv_bank[u][:, w, j * P : (j + 1) * P],
+                        words[:, 256 * g + w : 256 * (g + 1) : 2],
+                        ident_f32[:],
+                    )
+
+        def latent_regroup(u):
+            b, pair, g = latent_part(u)
+            if not 0 <= b < B:
+                return
+            cv_grouped[u] = work.tile([P, 2 * P * PACK], BF16, name="cv_grouped", align_bytes=64)
+            nc.scalar.copy(
+                out=cv_grouped[u][:].bitcast(F32).rearrange("p (c w) -> p c w", w=2),
+                in_=cv_bank[u][:].rearrange("p w c -> p c w"),
+            )
+
+        def latent_quantise(u):
+            b, pair, g = latent_part(u)
+            if not 0 <= b < B:
+                return
+            if pair == 0 and g == 0:
+                cv_codes[b] = work.tile([P, G, S], U32, name="cv_codes", align_bytes=64)
+                cv_scales[b] = work.tile([P, G, S], U8, name="cv_scales", align_bytes=64)
+            cols = slice(2 * P * pair, 2 * P * (pair + 1))
+            nc.vector.quantize_mx(
+                out=cv_codes[b][:, g, cols].bitcast(FP8X4),
+                scales=cv_scales[b][:, g, cols],
+                in_=cv_grouped[u][:],
+            )
+
+        def value_passes(u):
+            if not 0 <= u < UNITS:
+                return
+            b, h = divmod(u, H)
+            head = slice(h * DH, (h + 1) * DH)
+            v_bank[u] = ps_prep.tile([P, TILES, DH], F32, name="v_bank", tag="prep")
+            for j in range(TILES):
+                keys = slice(j * P, (j + 1) * P)
+                for g in range(G):
+                    nc.tensor.matmul_mx(
+                        out=v_bank[u][:, j, :],
+                        lhsT=cv_codes[b][:, g, keys].bitcast(FP8X4),
+                        lhsT_scale=cv_scales[b][:, g, keys],
+                        rhs=w_codes[:, g, head].bitcast(FP8X4),
+                        rhs_scale=w_scales[:, g, head],
+                        start=(g == 0),
+                        stop=(g == G - 1),
+                    )
+
+        def value_regroup(u):
+            if not 0 <= u < UNITS:
+                return
+            v_grouped[u] = work.tile([P, DH, PACK], BF16, name="v_grouped", align_bytes=64)
+            nc.scalar.copy(out=v_grouped[u][:], in_=v_bank[u][:].rearrange("p j d -> p d j"))
+
+        def value_quantise(u):
+            if not 0 <= u < UNITS:
+                return
+            v_codes[u] = work.tile([P, DH], U32, name="v_codes", bufs=3, align_bytes=64)
+            v_scales[u] = work.tile([P, DH], U8, name="v_scales", bufs=3, align_bytes=64)
+            nc.vector.quantize_mx(
+                out=v_codes[u][:].bitcast(FP8X4),
+                scales=v_scales[u][:],
+                in_=v_grouped[u][:].rearrange("p d j -> p (d j)"),
+            )
+
+        def score_matmul(n):
+            if not 0 <= n < UNITS * TILES:
+                return
+            u, t = divmod(n, TILES)
+            sc[n] = ps_scores.tile([P, S], F32, name="sc")
+            nc.tensor.matmul(
+                out=sc[n][:],
+                lhsT=qkT[u][:, 0, t * P : (t + 1) * P],
+                rhs=qkT[u][:, 1, :],
+                start=True,
+                stop=True,
+            )
+
+        def row_maximum(n):
+            if not 0 <= n < UNITS * TILES:
+                return
+            u, t = divmod(n, TILES)
+            if t == 0:
+                rowmax[u] = stats.tile([P, TILES], F32, name="rowmax")
+                bias[u] = stats.tile([P, TILES], F32, name="bias")
+            nc.vector.tensor_reduce(
+                out=rowmax[u][:, t : t + 1], in_=sc[n][:], axis=mybir.AxisListType.X, op=ALU.max
+            )
+            nc.gpsimd.tensor_scalar(
+                out=bias[u][:, t : t + 1],
+                in0=rowmax[u][:, t : t + 1],
+                scalar1=-SCALE,
+                scalar2=0.0,
+                op0=ALU.mult,
+                op1=ALU.add,
+            )
+
+        def exponentials(n):
+            if not 0 <= n < UNITS * TILES:
+                return
+            u, t = divmod(n, TILES)
+            if t == 0:
+                e[u] = work.tile([P, TILES, S], BF16, name="e", bufs=3)
+                rowsum[u] = stats.tile([P, TILES], F32, name="rowsum")
+            nc.scalar.activation(
+                out=e[u][:, t, :],
+                in_=sc[n][:],
+                func=mybir.ActivationFunctionType.Exp,
+                bias=bias[u][:, t : t + 1],
+                scale=SCALE,
+                accum_out=rowsum[u][:, t : t + 1],
+            )
+
+        def rowsum_reciprocal(u):
+            if not 0 <= u < UNITS:
+                return
+            recip[u] = stats.tile([P, TILES], F32, name="recip")
+            nc.vector.reciprocal(out=recip[u][:], in_=rowsum[u][:])
+
+        def e_transposes(u, half):
+            if not 0 <= u < UNITS:
+                return
+            eT_bank[u, half] = ps_eT.tile([P, 2, 2 * P], F32, name="eT_bank")
+            for j in range(2):
+                words = e[u][:, 2 * half + j, :].bitcast(F32)
+                for w in range(2):
+                    nc.tensor.transpose(
+                        eT_bank[u, half][:, w, j * P : (j + 1) * P],
+                        words[:, w * P : (w + 1) * P],
+                        ident_f32[:],
+                    )
+
+        def e_regroup(u, half):
+            if not 0 <= u < UNITS:
+                return
+            if half == 0:
+                e_grouped[u] = work.tile([P, S * PACK], BF16, name="e_grouped", align_bytes=64)
+            pairs = e_grouped[u][:].bitcast(F32).rearrange("p (c w) -> p c w", w=2)
+            dst = pairs[:, 2 * P * half : 2 * P * (half + 1), :]
+            src = eT_bank[u, half][:].rearrange("p w c -> p c w")
+            if half == 0:
+                nc.vector.tensor_copy(out=dst, in_=src)
+            else:
+                nc.scalar.copy(out=dst, in_=src)
+
+        def e_quantise(u):
+            if not 0 <= u < UNITS:
+                return
+            e_codes[u] = work.tile([P, S], U32, name="e_codes", align_bytes=64)
+            e_scales[u] = work.tile([P, S], U8, name="e_scales", align_bytes=64)
+            nc.vector.quantize_mx(
+                out=e_codes[u][:].bitcast(FP8X4), scales=e_scales[u][:], in_=e_grouped[u][:]
+            )
+
+        def context_passes(u):
+            if not 0 <= u < UNITS:
+                return
+            ctx_bank[u] = ps_ctx.tile([P, TILES, DH], F32, name="ctx_bank")
+            for t in range(TILES):
+                queries = slice(t * P, (t + 1) * P)
+                nc.tensor.matmul_mx(
+                    out=ctx_bank[u][:, t, :],
+                    lhsT=e_codes[u][:, queries].bitcast(FP8X4),
+                    lhsT_scale=e_scales[u][:, queries],
+                    rhs=v_codes[u][:].bitcast(FP8X4),
+                    rhs_scale=v_scales[u][:],
+                    start=True,
+                    stop=True,
+                )
+
+        def context_out(u):
+            if not 0 <= u < UNITS:
+                return
+            b, h = divmod(u, H)
+            result = work.tile([P, TILES, DH], F32, name="result", bufs=3)
+            nc.vector.tensor_tensor(
+                out=result[:],
+                in0=ctx_bank[u][:],
+                in1=recip[u][:].unsqueeze(2).to_broadcast([P, TILES, DH]),
+                op=ALU.mult,
+            )
+            nc.sync.dma_start(
+                out=out[b].rearrange("(p t) n -> p t n", t=TILES)[:, :, h * DH : (h + 1) * DH],
+                in_=result[:],
+            )
+
+        load_batch(0)
+        load_weight()
+        for n in range(-H * TILES, (UNITS + 1) * TILES + 1):
+            u, t = divmod(n, TILES)
+            exponentials(n)
+            if t == 0:
+                if u % H == 0:
+                    load_batch(u // H + 2)
+                e_transposes(u - 1, 1)
+                context_out(u - 2)
+                value_regroup(u - 1)
+            if t == 1:
+                qk_transposes(u)
+                latent_quantise(u - 1)
+                value_quantise(u - 1)
+                rowsum_reciprocal(u - 1)
+                e_regroup(u - 1, 1)
+            if t == 2:
+                e_transposes(u, 0)
+                latent_transposes(u)
+                e_quantise(u - 1)
+                qk_copy(u)
+            if t == 3:
+                context_passes(u - 1)
+                value_passes(u)
+                e_regroup(u, 0)
+                latent_regroup(u)
+            score_matmul(n + 3)
+            row_maximum(n + 2)

@@ -32,10 +32,8 @@ def tile_multiheadlatentattention_pb_t_kernel(
         inputs = ctx.enter_context(tc.tile_pool(name="inputs", bufs=3))
         work = ctx.enter_context(tc.tile_pool(name="work", bufs=2))
         stats = ctx.enter_context(tc.tile_pool(name="stats", bufs=4))
-        ps_scores = ctx.enter_context(tc.psum_pool(name="ps_scores", bufs=3))
-        ps_eT = ctx.enter_context(tc.psum_pool(name="ps_eT", bufs=2))
-        ps_ctx = ctx.enter_context(tc.psum_pool(name="ps_ctx", bufs=1))
-        ps_prep = ctx.enter_context(tc.psum_pool(name="ps_prep", bufs=2))
+        ps_scores = ctx.enter_context(tc.psum_pool(name="ps_scores", bufs=4))
+        ps_other = ctx.enter_context(tc.psum_pool(name="ps_other", bufs=4))
         ctx.enter_context(tc.manual_schedule())
 
         q_in, k_in, cv_in = {}, {}, {}
@@ -91,7 +89,7 @@ def tile_multiheadlatentattention_pb_t_kernel(
             if not 0 <= u + 2 < UNITS:
                 return
             b, h = divmod(u + 2, H)
-            qk_bank[u] = ps_prep.tile([P, 2, TILES, P], BF16, name="qk_bank", tag="prep")
+            qk_bank[u] = ps_other.tile([P, 2, TILES, P], BF16, name="qk_bank", tag="other")
             for t in range(TILES):
                 nc.tensor.transpose(
                     qk_bank[u][:, 0, t, :], q_in[b][:, t, h * DH : (h + 1) * DH], ident_bf16[:]
@@ -118,7 +116,7 @@ def tile_multiheadlatentattention_pb_t_kernel(
             b, pair, g = latent_part(u)
             if not 0 <= b < B:
                 return
-            cv_bank[u] = ps_prep.tile([P, 2, 2 * P], F32, name="cv_bank", tag="prep")
+            cv_bank[u] = ps_other.tile([P, 2, 2 * P], F32, name="cv_bank", tag="other")
             for j in range(2):
                 words = cv_in[b][:, 2 * pair + j, :].bitcast(F32)
                 for w in range(2):
@@ -157,7 +155,7 @@ def tile_multiheadlatentattention_pb_t_kernel(
                 return
             b, h = divmod(u, H)
             head = slice(h * DH, (h + 1) * DH)
-            v_bank[u] = ps_prep.tile([P, TILES, DH], F32, name="v_bank", tag="prep")
+            v_bank[u] = ps_other.tile([P, TILES, DH], F32, name="v_bank", tag="other")
             for j in range(TILES):
                 keys = slice(j * P, (j + 1) * P)
                 for g in range(G):
@@ -245,7 +243,7 @@ def tile_multiheadlatentattention_pb_t_kernel(
         def e_transposes(u, half):
             if not 0 <= u < UNITS:
                 return
-            eT_bank[u, half] = ps_eT.tile([P, 2, 2 * P], F32, name="eT_bank")
+            eT_bank[u, half] = ps_other.tile([P, 2, 2 * P], F32, name="eT_bank", tag="other")
             for j in range(2):
                 words = e[u][:, 2 * half + j, :].bitcast(F32)
                 for w in range(2):
@@ -280,7 +278,7 @@ def tile_multiheadlatentattention_pb_t_kernel(
         def context_passes(u):
             if not 0 <= u < UNITS:
                 return
-            ctx_bank[u] = ps_ctx.tile([P, TILES, DH], F32, name="ctx_bank")
+            ctx_bank[u] = ps_other.tile([P, TILES, DH], F32, name="ctx_bank", tag="other")
             for t in range(TILES):
                 queries = slice(t * P, (t + 1) * P)
                 nc.tensor.matmul_mx(
@@ -313,6 +311,8 @@ def tile_multiheadlatentattention_pb_t_kernel(
         load_weight()
         for n in range(-H * TILES, (UNITS + 1) * TILES + 1):
             u, t = divmod(n, TILES)
+            score_matmul(n + 3)
+            row_maximum(n + 2)
             exponentials(n)
             if t == 0:
                 if u % H == 0:
@@ -332,9 +332,7 @@ def tile_multiheadlatentattention_pb_t_kernel(
                 e_quantise(u - 1)
                 qk_copy(u)
             if t == 3:
-                context_passes(u - 1)
                 value_passes(u)
+                context_passes(u - 1)
                 e_regroup(u, 0)
                 latent_regroup(u)
-            score_matmul(n + 3)
-            row_maximum(n + 2)

@@ -34,7 +34,6 @@ def tile_multiheadlatentattention_pb_t_kernel(
         stats = ctx.enter_context(tc.tile_pool(name="stats", bufs=4))
         ps_scores = ctx.enter_context(tc.psum_pool(name="ps_scores", bufs=4))
         ps_other = ctx.enter_context(tc.psum_pool(name="ps_other", bufs=4))
-        ctx.enter_context(tc.manual_schedule())
 
         q_in, k_in, cv_in = {}, {}, {}
         qk_bank, qkT = {}, {}

@@ -34,6 +34,7 @@ def tile_multiheadlatentattention_pb_t_kernel(
         stats = ctx.enter_context(tc.tile_pool(name="stats", bufs=4))
         ps_scores = ctx.enter_context(tc.psum_pool(name="ps_scores", bufs=4))
         ps_other = ctx.enter_context(tc.psum_pool(name="ps_other", bufs=4))
+        ctx.enter_context(tc.manual_schedule())
 
         q_in, k_in, cv_in = {}, {}, {}
         qk_bank, qkT = {}, {}
@@ -55,19 +56,24 @@ def tile_multiheadlatentattention_pb_t_kernel(
             if not 0 <= b < B:
                 return
             cv_in[b] = inputs.tile([P, TILES, DV], BF16, name="cv_in")
-            for u in range(2):
-                nc.sync.dma_start(
-                    out=cv_in[b][:, 2 * u : 2 * u + 2, :],
-                    in_=c_v[b, 256 * u : 256 * (u + 1), :].rearrange("(p e) k -> p e k", e=2),
-                )
             q_in[b] = inputs.tile([P, TILES, H * DH], BF16, name="q_in")
-            nc.sync.dma_start(
-                out=q_in[b][:], in_=q_rot[b].rearrange("(p t) h d -> p t (h d)", t=TILES)
-            )
             k_in[b] = inputs.tile([P, TILES, H * DH], BF16, name="k_in")
-            nc.sync.dma_start(
-                out=k_in[b][:], in_=k_rot[b].rearrange("(t p) h d -> p t (h d)", p=P)
-            )
+            for half in range(2):
+                nc.sync.dma_start(
+                    out=cv_in[b][:, 2 * half : 2 * half + 2, :],
+                    in_=c_v[b, 256 * half : 256 * (half + 1), :].rearrange(
+                        "(p e) k -> p e k", e=2
+                    ),
+                )
+                heads = slice(2 * half * DH, 2 * (half + 1) * DH)
+                nc.sync.dma_start(
+                    out=q_in[b][:, :, heads],
+                    in_=q_rot[b].rearrange("(p t) h d -> p t (h d)", t=TILES)[:, :, heads],
+                )
+                nc.sync.dma_start(
+                    out=k_in[b][:, :, heads],
+                    in_=k_rot[b].rearrange("(t p) h d -> p t (h d)", p=P)[:, :, heads],
+                )
 
         def load_weight():
             for g in range(G):
@@ -130,7 +136,8 @@ def tile_multiheadlatentattention_pb_t_kernel(
             if not 0 <= b < B:
                 return
             cv_grouped[u] = work.tile([P, 2 * P * PACK], BF16, name="cv_grouped", align_bytes=64)
-            nc.scalar.copy(
+            copy = nc.vector.tensor_copy if u < 0 else nc.scalar.copy
+            copy(
                 out=cv_grouped[u][:].bitcast(F32).rearrange("p (c w) -> p c w", w=2),
                 in_=cv_bank[u][:].rearrange("p w c -> p c w"),
             )

@@ -20,6 +20,8 @@ G = DV // K_PASS
 TILES = S // P
 UNITS = B * H
 SCALE = 1.0 / math.sqrt(DH)
+FIRST_ON_VECTOR = (-3, -1)
+WARM = 5
 FLOPS = 2 * B * S * DV * H * DH + 4 * B * H * S * S * DH
 
 
@@ -44,6 +46,8 @@ def tile_multiheadlatentattention_pb_t_kernel(
         e, eT_bank, e_grouped, e_codes, e_scales = {}, {}, {}, {}, {}
         ctx_bank = {}
 
+        zeros = const.tile([P, S], BF16)
+        nc.vector.memset(zeros[:], 0.0)
         ident_f32 = const.tile([P, P], F32)
         make_identity(nc, ident_f32[:])
         ident_bf16 = const.tile([P, P], BF16)
@@ -52,20 +56,27 @@ def tile_multiheadlatentattention_pb_t_kernel(
         w_scales = const.tile([P, G, H * DH], U8, align_bytes=64)
         nc.vector.memset(w_scales[:].bitcast(I32), 0)
 
+        def warm_up(count):
+            for i in range(count):
+                idle = ps_scores.tile([P, S], F32, name="sc")
+                nc.tensor.matmul(out=idle[:], lhsT=zeros[:, 0:P], rhs=zeros[:], start=True, stop=True)
+
         def load_batch(b):
             if not 0 <= b < B:
                 return
             cv_in[b] = inputs.tile([P, TILES, DV], BF16, name="cv_in")
             q_in[b] = inputs.tile([P, TILES, H * DH], BF16, name="q_in")
             k_in[b] = inputs.tile([P, TILES, H * DH], BF16, name="k_in")
-            for half in range(2):
+            def load_latent(half):
                 nc.sync.dma_start(
                     out=cv_in[b][:, 2 * half : 2 * half + 2, :],
                     in_=c_v[b, 256 * half : 256 * (half + 1), :].rearrange(
                         "(p e) k -> p e k", e=2
                     ),
                 )
-                heads = slice(2 * half * DH, 2 * (half + 1) * DH)
+
+            def load_qk(first, count):
+                heads = slice(first * DH, (first + count) * DH)
                 nc.sync.dma_start(
                     out=q_in[b][:, :, heads],
                     in_=q_rot[b].rearrange("(p t) h d -> p t (h d)", t=TILES)[:, :, heads],
@@ -74,6 +85,17 @@ def tile_multiheadlatentattention_pb_t_kernel(
                     out=k_in[b][:, :, heads],
                     in_=k_rot[b].rearrange("(t p) h d -> p t (h d)", p=P)[:, :, heads],
                 )
+
+            if b == 0:
+                load_qk(0, 1)
+                load_qk(1, 1)
+                load_latent(0)
+                load_latent(1)
+                load_qk(2, 2)
+            else:
+                load_latent(0)
+                load_latent(1)
+                load_qk(0, H)
 
         def load_weight():
             for g in range(G):
@@ -90,26 +112,27 @@ def tile_multiheadlatentattention_pb_t_kernel(
                     ),
                 )
 
-        def qk_transposes(u):
+        def qk_transposes(u, parts=(0, 1)):
             if not 0 <= u + 2 < UNITS:
                 return
             b, h = divmod(u + 2, H)
-            qk_bank[u] = ps_other.tile([P, 2, TILES, P], BF16, name="qk_bank", tag="other")
-            for t in range(TILES):
-                nc.tensor.transpose(
-                    qk_bank[u][:, 0, t, :], q_in[b][:, t, h * DH : (h + 1) * DH], ident_bf16[:]
-                )
-            for t in range(TILES):
-                nc.tensor.transpose(
-                    qk_bank[u][:, 1, t, :], k_in[b][:, t, h * DH : (h + 1) * DH], ident_bf16[:]
-                )
+            bank = ps_other.tile([P, len(parts), TILES, P], BF16, name="qk_bank", tag="other")
+            qk_bank[u, parts] = bank
+            for i, w in enumerate(parts):
+                for t in range(TILES):
+                    nc.tensor.transpose(
+                        bank[:, i, t, :], (q_in, k_in)[w][b][:, t, h * DH : (h + 1) * DH], ident_bf16[:]
+                    )
 
-        def qk_copy(u):
+        def qk_copy(u, parts=(0, 1), engine="scalar"):
             if not 0 <= u + 2 < UNITS:
                 return
-            qkT[u + 2] = work.tile([P, 2, S], BF16, name="qkT", bufs=4)
-            nc.scalar.copy(
-                out=qkT[u + 2][:], in_=qk_bank[u][:].rearrange("p w t c -> p w (t c)")
+            if parts[0] == 0:
+                qkT[u + 2] = work.tile([P, 2, S], BF16, name="qkT", bufs=4)
+            copy = nc.vector.tensor_copy if engine == "vector" else nc.scalar.copy
+            copy(
+                out=qkT[u + 2][:, parts[0] : parts[0] + len(parts), :],
+                in_=qk_bank[u, parts][:].rearrange("p w t c -> p w (t c)"),
             )
 
         def latent_part(u):
@@ -136,7 +159,7 @@ def tile_multiheadlatentattention_pb_t_kernel(
             if not 0 <= b < B:
                 return
             cv_grouped[u] = work.tile([P, 2 * P * PACK], BF16, name="cv_grouped", align_bytes=64)
-            copy = nc.vector.tensor_copy if u < 0 else nc.scalar.copy
+            copy = nc.vector.tensor_copy if u in FIRST_ON_VECTOR else nc.scalar.copy
             copy(
                 out=cv_grouped[u][:].bitcast(F32).rearrange("p (c w) -> p c w", w=2),
                 in_=cv_bank[u][:].rearrange("p w c -> p c w"),
@@ -175,11 +198,12 @@ def tile_multiheadlatentattention_pb_t_kernel(
                         stop=(g == G - 1),
                     )
 
-        def value_regroup(u):
+        def value_regroup(u, engine="scalar"):
             if not 0 <= u < UNITS:
                 return
             v_grouped[u] = work.tile([P, DH, PACK], BF16, name="v_grouped", align_bytes=64)
-            nc.scalar.copy(out=v_grouped[u][:], in_=v_bank[u][:].rearrange("p j d -> p d j"))
+            copy = nc.vector.tensor_copy if engine == "vector" else nc.scalar.copy
+            copy(out=v_grouped[u][:], in_=v_bank[u][:].rearrange("p j d -> p d j"))
 
         def value_quantise(u):
             if not 0 <= u < UNITS:
@@ -246,49 +270,57 @@ def tile_multiheadlatentattention_pb_t_kernel(
             recip[u] = stats.tile([P, TILES], F32, name="recip")
             nc.vector.reciprocal(out=recip[u][:], in_=rowsum[u][:])
 
-        def e_transposes(u, half):
+        def e_transposes(u, piece):
             if not 0 <= u < UNITS:
                 return
-            eT_bank[u, half] = ps_other.tile([P, 2, 2 * P], F32, name="eT_bank", tag="other")
-            for j in range(2):
-                words = e[u][:, 2 * half + j, :].bitcast(F32)
+            first, count = piece
+            eT_bank[u, first] = ps_other.tile([P, 2, count * P], F32, name="eT_bank", tag="other")
+            for j in range(count):
+                words = e[u][:, first + j, :].bitcast(F32)
                 for w in range(2):
                     nc.tensor.transpose(
-                        eT_bank[u, half][:, w, j * P : (j + 1) * P],
+                        eT_bank[u, first][:, w, j * P : (j + 1) * P],
                         words[:, w * P : (w + 1) * P],
                         ident_f32[:],
                     )
 
-        def e_regroup(u, half):
+        def e_regroup(u, piece, engine):
             if not 0 <= u < UNITS:
                 return
-            if half == 0:
+            first, count = piece
+            if first == 0:
                 e_grouped[u] = work.tile([P, S * PACK], BF16, name="e_grouped", align_bytes=64)
             pairs = e_grouped[u][:].bitcast(F32).rearrange("p (c w) -> p c w", w=2)
-            dst = pairs[:, 2 * P * half : 2 * P * (half + 1), :]
-            src = eT_bank[u, half][:].rearrange("p w c -> p c w")
-            if half == 0:
+            dst = pairs[:, P * first : P * (first + count), :]
+            src = eT_bank[u, first][:].rearrange("p w c -> p c w")
+            if engine == "vector":
                 nc.vector.tensor_copy(out=dst, in_=src)
             else:
                 nc.scalar.copy(out=dst, in_=src)
 
-        def e_quantise(u):
+        def e_quantise(u, piece):
             if not 0 <= u < UNITS:
                 return
-            e_codes[u] = work.tile([P, S], U32, name="e_codes", align_bytes=64)
-            e_scales[u] = work.tile([P, S], U8, name="e_scales", align_bytes=64)
+            first, count = piece
+            if first == 0:
+                e_codes[u] = work.tile([P, S], U32, name="e_codes", align_bytes=64)
+                e_scales[u] = work.tile([P, S], U8, name="e_scales", align_bytes=64)
+            cols = slice(P * first, P * (first + count))
             nc.vector.quantize_mx(
-                out=e_codes[u][:].bitcast(FP8X4), scales=e_scales[u][:], in_=e_grouped[u][:]
+                out=e_codes[u][:, cols].bitcast(FP8X4),
+                scales=e_scales[u][:, cols],
+                in_=e_grouped[u][:, PACK * P * first : PACK * P * (first + count)],
             )
 
-        def context_passes(u):
+        def context_passes(u, piece):
             if not 0 <= u < UNITS:
                 return
-            ctx_bank[u] = ps_other.tile([P, TILES, DH], F32, name="ctx_bank", tag="other")
-            for t in range(TILES):
-                queries = slice(t * P, (t + 1) * P)
+            first, count = piece
+            ctx_bank[u, first] = ps_other.tile([P, count, DH], F32, name="ctx_bank", tag="other")
+            for j in range(count):
+                queries = slice((first + j) * P, (first + j + 1) * P)
                 nc.tensor.matmul_mx(
-                    out=ctx_bank[u][:, t, :],
+                    out=ctx_bank[u, first][:, j, :],
                     lhsT=e_codes[u][:, queries].bitcast(FP8X4),
                     lhsT_scale=e_scales[u][:, queries],
                     rhs=v_codes[u][:].bitcast(FP8X4),
@@ -297,48 +329,140 @@ def tile_multiheadlatentattention_pb_t_kernel(
                     stop=True,
                 )
 
-        def context_out(u):
+        def context_out(u, piece, engine="vector"):
             if not 0 <= u < UNITS:
                 return
             b, h = divmod(u, H)
-            result = work.tile([P, TILES, DH], F32, name="result", bufs=3)
-            nc.vector.tensor_tensor(
-                out=result[:],
-                in0=ctx_bank[u][:],
-                in1=recip[u][:].unsqueeze(2).to_broadcast([P, TILES, DH]),
-                op=ALU.mult,
-            )
+            first, count = piece
+            result = work.tile([P, count, DH], F32, name="result", bufs=6)
+            if engine == "vector":
+                nc.vector.tensor_tensor(
+                    out=result[:],
+                    in0=ctx_bank[u, first][:],
+                    in1=recip[u][:, first : first + count].unsqueeze(2).to_broadcast([P, count, DH]),
+                    op=ALU.mult,
+                )
+            else:
+                for j in range(count):
+                    nc.scalar.activation(
+                        out=result[:, j, :],
+                        in_=ctx_bank[u, first][:, j, :],
+                        func=mybir.ActivationFunctionType.Copy,
+                        scale=recip[u][:, first + j : first + j + 1],
+                    )
             nc.sync.dma_start(
-                out=out[b].rearrange("(p t) n -> p t n", t=TILES)[:, :, h * DH : (h + 1) * DH],
+                out=out[b].rearrange("(p t) n -> p t n", t=TILES)[
+                    :, first : first + count, h * DH : (h + 1) * DH
+                ],
                 in_=result[:],
             )
 
+        FRONT, BACK, WHOLE = (0, 2), (2, 2), (0, TILES)
+        LAST = UNITS - 1
         load_batch(0)
         load_weight()
-        for n in range(-H * TILES, (UNITS + 1) * TILES + 1):
+        load_batch(1)
+        warm_up(WARM)
+        qk_transposes(-2, (0,))
+        qk_copy(-2, (0,), "scalar")
+        qk_transposes(-2, (1,))
+        qk_copy(-2, (1,), "vector")
+        for n in range(TILES):
+            score_matmul(n)
+        row_maximum(0)
+        row_maximum(1)
+        qk_transposes(-1)
+        qk_copy(-1)
+        row_maximum(2)
+        row_maximum(3)
+        exponentials(0)
+        load_batch(2)
+        latent_transposes(-4)
+        latent_transposes(-3)
+        score_matmul(4)
+        exponentials(1)
+        latent_regroup(-4)
+        latent_regroup(-3)
+        latent_transposes(-2)
+        latent_transposes(-1)
+        score_matmul(5)
+        row_maximum(4)
+        exponentials(2)
+        latent_quantise(-4)
+        latent_quantise(-3)
+        latent_regroup(-2)
+        latent_regroup(-1)
+        e_transposes(0, FRONT)
+        score_matmul(6)
+        row_maximum(5)
+        exponentials(3)
+        latent_quantise(-2)
+        latent_quantise(-1)
+        qk_transposes(0)
+        value_passes(0)
+        e_regroup(0, FRONT, "vector")
+        qk_copy(0)
+        for n in range(TILES, LAST * TILES + 1):
             u, t = divmod(n, TILES)
             score_matmul(n + 3)
             row_maximum(n + 2)
             exponentials(n)
+            if n == TILES + 1:
+                latent_transposes(0)
+            if n == TILES + 2:
+                latent_regroup(0)
+            if n == TILES + 3:
+                latent_quantise(0)
             if t == 0:
                 if u % H == 0:
                     load_batch(u // H + 2)
-                e_transposes(u - 1, 1)
-                context_out(u - 2)
+                e_transposes(u - 1, BACK)
+                context_out(u - 2, WHOLE)
                 value_regroup(u - 1)
             if t == 1:
                 qk_transposes(u)
-                latent_quantise(u - 1)
+                if u > 1:
+                    latent_quantise(u - 1)
                 value_quantise(u - 1)
                 rowsum_reciprocal(u - 1)
-                e_regroup(u - 1, 1)
+                e_regroup(u - 1, BACK, "scalar")
             if t == 2:
-                e_transposes(u, 0)
+                e_transposes(u, FRONT)
                 latent_transposes(u)
-                e_quantise(u - 1)
+                e_quantise(u - 1, WHOLE)
                 qk_copy(u)
             if t == 3:
                 value_passes(u)
-                context_passes(u - 1)
-                e_regroup(u, 0)
+                context_passes(u - 1, WHOLE)
+                e_regroup(u, FRONT, "vector" if u + 2 < UNITS else "scalar")
                 latent_regroup(u)
+        n = LAST * TILES
+        value_passes(LAST)
+        row_maximum(n + 3)
+        exponentials(n + 1)
+        value_quantise(LAST - 1)
+        rowsum_reciprocal(LAST - 1)
+        e_regroup(LAST - 1, BACK, "scalar")
+        exponentials(n + 2)
+        e_transposes(LAST, FRONT)
+        value_regroup(LAST, "vector")
+        e_quantise(LAST - 1, WHOLE)
+        exponentials(n + 3)
+        e_transposes(LAST, (2, 1))
+        e_regroup(LAST, FRONT, "vector")
+        context_passes(LAST - 1, WHOLE)
+        value_quantise(LAST)
+        e_regroup(LAST, (2, 1), "vector")
+        e_transposes(LAST, (3, 1))
+        e_quantise(LAST, FRONT)
+        rowsum_reciprocal(LAST)
+        e_regroup(LAST, (3, 1), "scalar")
+        context_out(LAST - 1, WHOLE, "scalar")
+        context_passes(LAST, FRONT)
+        e_quantise(LAST, (2, 1))
+        e_quantise(LAST, (3, 1))
+        context_passes(LAST, (2, 1))
+        context_out(LAST, FRONT, "vector")
+        context_passes(LAST, (3, 1))
+        context_out(LAST, (2, 1), "scalar")
+        context_out(LAST, (3, 1), "vector")

@@ -48,10 +48,10 @@ def tile_multiheadlatentattention_pb_t_kernel(
 
         zeros = const.tile([P, S], BF16)
         nc.vector.memset(zeros[:], 0.0)
-        ident_f32 = const.tile([P, P], F32)
-        make_identity(nc, ident_f32[:])
         ident_bf16 = const.tile([P, P], BF16)
         make_identity(nc, ident_bf16[:])
+        ident_f32 = const.tile([P, P], F32)
+        make_identity(nc, ident_f32[:])
         w_codes = const.tile([P, G, H * DH], U32, align_bytes=64)
         w_scales = const.tile([P, G, H * DH], U8, align_bytes=64)
         nc.vector.memset(w_scales[:].bitcast(I32), 0)
@@ -450,19 +450,19 @@ def tile_multiheadlatentattention_pb_t_kernel(
         exponentials(n + 3)
         e_transposes(LAST, (2, 1))
         e_regroup(LAST, FRONT, "vector")
-        context_passes(LAST - 1, WHOLE)
-        value_quantise(LAST)
-        e_regroup(LAST, (2, 1), "vector")
         e_transposes(LAST, (3, 1))
+        e_regroup(LAST, (2, 1), "scalar")
+        e_regroup(LAST, (3, 1), "scalar")
+        value_quantise(LAST)
         e_quantise(LAST, FRONT)
         rowsum_reciprocal(LAST)
-        e_regroup(LAST, (3, 1), "scalar")
-        context_out(LAST - 1, WHOLE, "scalar")
-        context_passes(LAST, FRONT)
         e_quantise(LAST, (2, 1))
         e_quantise(LAST, (3, 1))
+        context_passes(LAST - 1, WHOLE)
+        context_passes(LAST, FRONT)
         context_passes(LAST, (2, 1))
-        context_out(LAST, FRONT, "vector")
         context_passes(LAST, (3, 1))
+        context_out(LAST - 1, WHOLE, "scalar")
+        context_out(LAST, FRONT, "vector")
         context_out(LAST, (2, 1), "scalar")
         context_out(LAST, (3, 1), "vector")

@@ -22,6 +22,7 @@ UNITS = B * H
 SCALE = 1.0 / math.sqrt(DH)
 FIRST_ON_VECTOR = (-3, -1)
 WARM = 5
+OWN = (0, 1, 2, 3) + tuple(range(UNITS * TILES - 8, UNITS * TILES))
 FLOPS = 2 * B * S * DV * H * DH + 4 * B * H * S * S * DH
 
 
@@ -45,6 +46,7 @@ def tile_multiheadlatentattention_pb_t_kernel(
         sc, rowmax, bias, rowsum, recip = {}, {}, {}, {}, {}
         e, eT_bank, e_grouped, e_codes, e_scales = {}, {}, {}, {}, {}
         ctx_bank = {}
+        own_bias = {}
 
         zeros = const.tile([P, S], BF16)
         nc.vector.memset(zeros[:], 0.0)
@@ -236,6 +238,19 @@ def tile_multiheadlatentattention_pb_t_kernel(
             if t == 0:
                 rowmax[u] = stats.tile([P, TILES], F32, name="rowmax")
                 bias[u] = stats.tile([P, TILES], F32, name="bias")
+            if n in OWN:
+                scaled = work.tile([P, S], BF16, name="scaled")
+                own_bias[n] = stats.tile([P, 1], F32, name="own_bias")
+                nc.vector.tensor_scalar(
+                    out=scaled[:],
+                    in0=sc[n][:],
+                    scalar1=-SCALE,
+                    scalar2=None,
+                    op0=ALU.mult,
+                    op1=ALU.min,
+                    accum_out=own_bias[n][:],
+                )
+                return
             nc.vector.tensor_reduce(
                 out=rowmax[u][:, t : t + 1], in_=sc[n][:], axis=mybir.AxisListType.X, op=ALU.max
             )
@@ -259,7 +274,7 @@ def tile_multiheadlatentattention_pb_t_kernel(
                 out=e[u][:, t, :],
                 in_=sc[n][:],
                 func=mybir.ActivationFunctionType.Exp,
-                bias=bias[u][:, t : t + 1],
+                bias=own_bias[n][:] if n in OWN else bias[u][:, t : t + 1],
                 scale=SCALE,
                 accum_out=rowsum[u][:, t : t + 1],
             )
@@ -372,10 +387,10 @@ def tile_multiheadlatentattention_pb_t_kernel(
         row_maximum(0)
         row_maximum(1)
         qk_transposes(-1)
+        exponentials(0)
         qk_copy(-1)
         row_maximum(2)
         row_maximum(3)
-        exponentials(0)
         load_batch(2)
         latent_transposes(-4)
         latent_transposes(-3)

import math
from contextlib import ExitStack

import concourse.mybir as mybir
from concourse.masks import make_identity

F32 = mybir.dt.float32
BF16 = mybir.dt.bfloat16
U32 = mybir.dt.uint32
U8 = mybir.dt.uint8
I32 = mybir.dt.int32
FP8X4 = mybir.dt.float8_e4m3fn_x4
ALU = mybir.AluOpType

B, S, H, DH, DV = 8, 512, 4, 128, 1024
P = 128
PACK = 4
K_PASS = P * PACK
G = DV // K_PASS
TILES = S // P
UNITS = B * H
SCALE = 1.0 / math.sqrt(DH)
FIRST_ON_VECTOR = (-3, -1)
WARM = 5
OWN = (0, 1, 2, 3) + tuple(range(UNITS * TILES - 8, UNITS * TILES))
FLOPS = 2 * B * S * DV * H * DH + 4 * B * H * S * S * DH


def tile_multiheadlatentattention_pb_t_kernel(
    tc, q_rot, k_rot, c_v, W_v_dec_words, W_v_dec_scales, out
):
    nc = tc.nc
    with ExitStack() as ctx:
        const = ctx.enter_context(tc.tile_pool(name="const", bufs=1))
        inputs = ctx.enter_context(tc.tile_pool(name="inputs", bufs=3))
        work = ctx.enter_context(tc.tile_pool(name="work", bufs=2))
        stats = ctx.enter_context(tc.tile_pool(name="stats", bufs=4))
        ps_scores = ctx.enter_context(tc.psum_pool(name="ps_scores", bufs=4))
        ps_other = ctx.enter_context(tc.psum_pool(name="ps_other", bufs=4))
        ctx.enter_context(tc.manual_schedule())

        q_in, k_in, cv_in = {}, {}, {}
        qk_bank, qkT = {}, {}
        cv_bank, cv_grouped, cv_codes, cv_scales = {}, {}, {}, {}
        v_bank, v_grouped, v_codes, v_scales = {}, {}, {}, {}
        sc, rowmax, bias, rowsum, recip = {}, {}, {}, {}, {}
        e, eT_bank, e_grouped, e_codes, e_scales = {}, {}, {}, {}, {}
        ctx_bank = {}
        own_bias = {}

        zeros = const.tile([P, S], BF16)
        nc.vector.memset(zeros[:], 0.0)
        ident_bf16 = const.tile([P, P], BF16)
        make_identity(nc, ident_bf16[:])
        ident_f32 = const.tile([P, P], F32)
        make_identity(nc, ident_f32[:])
        w_codes = const.tile([P, G, H * DH], U32, align_bytes=64)
        w_scales = const.tile([P, G, H * DH], U8, align_bytes=64)
        nc.vector.memset(w_scales[:].bitcast(I32), 0)

        def warm_up(count):
            for i in range(count):
                idle = ps_scores.tile([P, S], F32, name="sc")
                nc.tensor.matmul(out=idle[:], lhsT=zeros[:, 0:P], rhs=zeros[:], start=True, stop=True)

        def load_batch(b):
            if not 0 <= b < B:
                return
            cv_in[b] = inputs.tile([P, TILES, DV], BF16, name="cv_in")
            q_in[b] = inputs.tile([P, TILES, H * DH], BF16, name="q_in")
            k_in[b] = inputs.tile([P, TILES, H * DH], BF16, name="k_in")
            def load_latent(half):
                nc.sync.dma_start(
                    out=cv_in[b][:, 2 * half : 2 * half + 2, :],
                    in_=c_v[b, 256 * half : 256 * (half + 1), :].rearrange(
                        "(p e) k -> p e k", e=2
                    ),
                )

            def load_qk(first, count):
                heads = slice(first * DH, (first + count) * DH)
                nc.sync.dma_start(
                    out=q_in[b][:, :, heads],
                    in_=q_rot[b].rearrange("(p t) h d -> p t (h d)", t=TILES)[:, :, heads],
                )
                nc.sync.dma_start(
                    out=k_in[b][:, :, heads],
                    in_=k_rot[b].rearrange("(t p) h d -> p t (h d)", p=P)[:, :, heads],
                )

            if b == 0:
                load_qk(0, 1)
                load_qk(1, 1)
                load_latent(0)
                load_latent(1)
                load_qk(2, 2)
            else:
                load_latent(0)
                load_latent(1)
                load_qk(0, H)

        def load_weight():
            for g in range(G):
                nc.sync.dma_start(
                    out=w_codes[:, g, :].bitcast(I32),
                    in_=W_v_dec_words[g].rearrange("p n t -> p (n t)").bitcast(I32),
                )
            scale_rows = W_v_dec_scales.bitcast(I32)
            for quadrant in range(4):
                nc.sync.dma_start(
                    out=w_scales[32 * quadrant : 32 * quadrant + 4, :, :].bitcast(I32),
                    in_=scale_rows[:, 4 * quadrant : 4 * quadrant + 4, :].rearrange(
                        "g r n -> r g n"
                    ),
                )

        def qk_transposes(u, parts=(0, 1)):
            if not 0 <= u + 2 < UNITS:
                return
            b, h = divmod(u + 2, H)
            bank = ps_other.tile([P, len(parts), TILES, P], BF16, name="qk_bank", tag="other")
            qk_bank[u, parts] = bank
            for i, w in enumerate(parts):
                for t in range(TILES):
                    nc.tensor.transpose(
                        bank[:, i, t, :], (q_in, k_in)[w][b][:, t, h * DH : (h + 1) * DH], ident_bf16[:]
                    )

        def qk_copy(u, parts=(0, 1), engine="scalar"):
            if not 0 <= u + 2 < UNITS:
                return
            if parts[0] == 0:
                qkT[u + 2] = work.tile([P, 2, S], BF16, name="qkT", bufs=4)
            copy = nc.vector.tensor_copy if engine == "vector" else nc.scalar.copy
            copy(
                out=qkT[u + 2][:, parts[0] : parts[0] + len(parts), :],
                in_=qk_bank[u, parts][:].rearrange("p w t c -> p w (t c)"),
            )

        def latent_part(u):
            b, part = divmod(u + H, H)
            pair, g = divmod(part, G)
            return b, pair, g

        def latent_transposes(u):
            b, pair, g = latent_part(u)
            if not 0 <= b < B:
                return
            cv_bank[u] = ps_other.tile([P, 2, 2 * P], F32, name="cv_bank", tag="other")
            for j in range(2):
                words = cv_in[b][:, 2 * pair + j, :].bitcast(F32)
                for w in range(2):
                    nc.tensor.transpose(
                        cv_bank[u][:, w, j * P : (j + 1) * P],
                        words[:, 256 * g + w : 256 * (g + 1) : 2],
                        ident_f32[:],
                    )

        def latent_regroup(u):
            b, pair, g = latent_part(u)
            if not 0 <= b < B:
                return
            cv_grouped[u] = work.tile([P, 2 * P * PACK], BF16, name="cv_grouped", align_bytes=64)
            copy = nc.vector.tensor_copy if u in FIRST_ON_VECTOR else nc.scalar.copy
            copy(
                out=cv_grouped[u][:].bitcast(F32).rearrange("p (c w) -> p c w", w=2),
                in_=cv_bank[u][:].rearrange("p w c -> p c w"),
            )

        def latent_quantise(u):
            b, pair, g = latent_part(u)
            if not 0 <= b < B:
                return
            if pair == 0 and g == 0:
                cv_codes[b] = work.tile([P, G, S], U32, name="cv_codes", align_bytes=64)
                cv_scales[b] = work.tile([P, G, S], U8, name="cv_scales", align_bytes=64)
            cols = slice(2 * P * pair, 2 * P * (pair + 1))
            nc.vector.quantize_mx(
                out=cv_codes[b][:, g, cols].bitcast(FP8X4),
                scales=cv_scales[b][:, g, cols],
                in_=cv_grouped[u][:],
            )

        def value_passes(u):
            if not 0 <= u < UNITS:
                return
            b, h = divmod(u, H)
            head = slice(h * DH, (h + 1) * DH)
            v_bank[u] = ps_other.tile([P, TILES, DH], F32, name="v_bank", tag="other")
            for j in range(TILES):
                keys = slice(j * P, (j + 1) * P)
                for g in range(G):
                    nc.tensor.matmul_mx(
                        out=v_bank[u][:, j, :],
                        lhsT=cv_codes[b][:, g, keys].bitcast(FP8X4),
                        lhsT_scale=cv_scales[b][:, g, keys],
                        rhs=w_codes[:, g, head].bitcast(FP8X4),
                        rhs_scale=w_scales[:, g, head],
                        start=(g == 0),
                        stop=(g == G - 1),
                    )

        def value_regroup(u, engine="scalar"):
            if not 0 <= u < UNITS:
                return
            v_grouped[u] = work.tile([P, DH, PACK], BF16, name="v_grouped", align_bytes=64)
            copy = nc.vector.tensor_copy if engine == "vector" else nc.scalar.copy
            copy(out=v_grouped[u][:], in_=v_bank[u][:].rearrange("p j d -> p d j"))

        def value_quantise(u):
            if not 0 <= u < UNITS:
                return
            v_codes[u] = work.tile([P, DH], U32, name="v_codes", bufs=3, align_bytes=64)
            v_scales[u] = work.tile([P, DH], U8, name="v_scales", bufs=3, align_bytes=64)
            nc.vector.quantize_mx(
                out=v_codes[u][:].bitcast(FP8X4),
                scales=v_scales[u][:],
                in_=v_grouped[u][:].rearrange("p d j -> p (d j)"),
            )

        def score_matmul(n):
            if not 0 <= n < UNITS * TILES:
                return
            u, t = divmod(n, TILES)
            sc[n] = ps_scores.tile([P, S], F32, name="sc")
            nc.tensor.matmul(
                out=sc[n][:],
                lhsT=qkT[u][:, 0, t * P : (t + 1) * P],
                rhs=qkT[u][:, 1, :],
                start=True,
                stop=True,
            )

        def row_maximum(n):
            if not 0 <= n < UNITS * TILES:
                return
            u, t = divmod(n, TILES)
            if t == 0:
                rowmax[u] = stats.tile([P, TILES], F32, name="rowmax")
                bias[u] = stats.tile([P, TILES], F32, name="bias")
            if n in OWN:
                scaled = work.tile([P, S], BF16, name="scaled")
                own_bias[n] = stats.tile([P, 1], F32, name="own_bias")
                nc.vector.tensor_scalar(
                    out=scaled[:],
                    in0=sc[n][:],
                    scalar1=-SCALE,
                    scalar2=None,
                    op0=ALU.mult,
                    op1=ALU.min,
                    accum_out=own_bias[n][:],
                )
                return
            nc.vector.tensor_reduce(
                out=rowmax[u][:, t : t + 1], in_=sc[n][:], axis=mybir.AxisListType.X, op=ALU.max
            )
            nc.gpsimd.tensor_scalar(
                out=bias[u][:, t : t + 1],
                in0=rowmax[u][:, t : t + 1],
                scalar1=-SCALE,
                scalar2=0.0,
                op0=ALU.mult,
                op1=ALU.add,
            )

        def exponentials(n):
            if not 0 <= n < UNITS * TILES:
                return
            u, t = divmod(n, TILES)
            if t == 0:
                e[u] = work.tile([P, TILES, S], BF16, name="e", bufs=3)
                rowsum[u] = stats.tile([P, TILES], F32, name="rowsum")
            nc.scalar.activation(
                out=e[u][:, t, :],
                in_=sc[n][:],
                func=mybir.ActivationFunctionType.Exp,
                bias=own_bias[n][:] if n in OWN else bias[u][:, t : t + 1],
                scale=SCALE,
                accum_out=rowsum[u][:, t : t + 1],
            )

        def rowsum_reciprocal(u):
            if not 0 <= u < UNITS:
                return
            recip[u] = stats.tile([P, TILES], F32, name="recip")
            nc.vector.reciprocal(out=recip[u][:], in_=rowsum[u][:])

        def e_transposes(u, piece):
            if not 0 <= u < UNITS:
                return
            first, count = piece
            eT_bank[u, first] = ps_other.tile([P, 2, count * P], F32, name="eT_bank", tag="other")
            for j in range(count):
                words = e[u][:, first + j, :].bitcast(F32)
                for w in range(2):
                    nc.tensor.transpose(
                        eT_bank[u, first][:, w, j * P : (j + 1) * P],
                        words[:, w * P : (w + 1) * P],
                        ident_f32[:],
                    )

        def e_regroup(u, piece, engine):
            if not 0 <= u < UNITS:
                return
            first, count = piece
            if first == 0:
                e_grouped[u] = work.tile([P, S * PACK], BF16, name="e_grouped", align_bytes=64)
            pairs = e_grouped[u][:].bitcast(F32).rearrange("p (c w) -> p c w", w=2)
            dst = pairs[:, P * first : P * (first + count), :]
            src = eT_bank[u, first][:].rearrange("p w c -> p c w")
            if engine == "vector":
                nc.vector.tensor_copy(out=dst, in_=src)
            else:
                nc.scalar.copy(out=dst, in_=src)

        def e_quantise(u, piece):
            if not 0 <= u < UNITS:
                return
            first, count = piece
            if first == 0:
                e_codes[u] = work.tile([P, S], U32, name="e_codes", align_bytes=64)
                e_scales[u] = work.tile([P, S], U8, name="e_scales", align_bytes=64)
            cols = slice(P * first, P * (first + count))
            nc.vector.quantize_mx(
                out=e_codes[u][:, cols].bitcast(FP8X4),
                scales=e_scales[u][:, cols],
                in_=e_grouped[u][:, PACK * P * first : PACK * P * (first + count)],
            )

        def context_passes(u, piece):
            if not 0 <= u < UNITS:
                return
            first, count = piece
            ctx_bank[u, first] = ps_other.tile([P, count, DH], F32, name="ctx_bank", tag="other")
            for j in range(count):
                queries = slice((first + j) * P, (first + j + 1) * P)
                nc.tensor.matmul_mx(
                    out=ctx_bank[u, first][:, j, :],
                    lhsT=e_codes[u][:, queries].bitcast(FP8X4),
                    lhsT_scale=e_scales[u][:, queries],
                    rhs=v_codes[u][:].bitcast(FP8X4),
                    rhs_scale=v_scales[u][:],
                    start=True,
                    stop=True,
                )

        def context_out(u, piece, engine="vector"):
            if not 0 <= u < UNITS:
                return
            b, h = divmod(u, H)
            first, count = piece
            result = work.tile([P, count, DH], F32, name="result", bufs=6)
            if engine == "vector":
                nc.vector.tensor_tensor(
                    out=result[:],
                    in0=ctx_bank[u, first][:],
                    in1=recip[u][:, first : first + count].unsqueeze(2).to_broadcast([P, count, DH]),
                    op=ALU.mult,
                )
            else:
                for j in range(count):
                    nc.scalar.activation(
                        out=result[:, j, :],
                        in_=ctx_bank[u, first][:, j, :],
                        func=mybir.ActivationFunctionType.Copy,
                        scale=recip[u][:, first + j : first + j + 1],
                    )
            nc.sync.dma_start(
                out=out[b].rearrange("(p t) n -> p t n", t=TILES)[
                    :, first : first + count, h * DH : (h + 1) * DH
                ],
                in_=result[:],
            )

        FRONT, BACK, WHOLE = (0, 2), (2, 2), (0, TILES)
        LAST = UNITS - 1
        load_batch(0)
        load_weight()
        load_batch(1)
        warm_up(WARM)
        qk_transposes(-2, (0,))
        qk_copy(-2, (0,), "scalar")
        qk_transposes(-2, (1,))
        qk_copy(-2, (1,), "vector")
        for n in range(TILES):
            score_matmul(n)
        row_maximum(0)
        row_maximum(1)
        qk_transposes(-1)
        exponentials(0)
        qk_copy(-1)
        row_maximum(2)
        row_maximum(3)
        load_batch(2)
        latent_transposes(-4)
        latent_transposes(-3)
        score_matmul(4)
        exponentials(1)
        latent_regroup(-4)
        latent_regroup(-3)
        latent_transposes(-2)
        latent_transposes(-1)
        score_matmul(5)
        row_maximum(4)
        exponentials(2)
        latent_quantise(-4)
        latent_quantise(-3)
        latent_regroup(-2)
        latent_regroup(-1)
        e_transposes(0, FRONT)
        score_matmul(6)
        row_maximum(5)
        exponentials(3)
        latent_quantise(-2)
        latent_quantise(-1)
        qk_transposes(0)
        value_passes(0)
        e_regroup(0, FRONT, "vector")
        qk_copy(0)
        for n in range(TILES, LAST * TILES + 1):
            u, t = divmod(n, TILES)
            score_matmul(n + 3)
            row_maximum(n + 2)
            exponentials(n)
            if n == TILES + 1:
                latent_transposes(0)
            if n == TILES + 2:
                latent_regroup(0)
            if n == TILES + 3:
                latent_quantise(0)
            if t == 0:
                if u % H == 0:
                    load_batch(u // H + 2)
                e_transposes(u - 1, BACK)
                context_out(u - 2, WHOLE)
                value_regroup(u - 1)
            if t == 1:
                qk_transposes(u)
                if u > 1:
                    latent_quantise(u - 1)
                value_quantise(u - 1)
                rowsum_reciprocal(u - 1)
                e_regroup(u - 1, BACK, "scalar")
            if t == 2:
                e_transposes(u, FRONT)
                latent_transposes(u)
                e_quantise(u - 1, WHOLE)
                qk_copy(u)
            if t == 3:
                value_passes(u)
                context_passes(u - 1, WHOLE)
                e_regroup(u, FRONT, "vector" if u + 2 < UNITS else "scalar")
                latent_regroup(u)
        n = LAST * TILES
        value_passes(LAST)
        row_maximum(n + 3)
        exponentials(n + 1)
        value_quantise(LAST - 1)
        rowsum_reciprocal(LAST - 1)
        e_regroup(LAST - 1, BACK, "scalar")
        exponentials(n + 2)
        e_transposes(LAST, FRONT)
        value_regroup(LAST, "vector")
        e_quantise(LAST - 1, WHOLE)
        exponentials(n + 3)
        e_transposes(LAST, (2, 1))
        e_regroup(LAST, FRONT, "vector")
        e_transposes(LAST, (3, 1))
        e_regroup(LAST, (2, 1), "scalar")
        e_regroup(LAST, (3, 1), "scalar")
        value_quantise(LAST)
        e_quantise(LAST, FRONT)
        rowsum_reciprocal(LAST)
        e_quantise(LAST, (2, 1))
        e_quantise(LAST, (3, 1))
        context_passes(LAST - 1, WHOLE)
        context_passes(LAST, FRONT)
        context_passes(LAST, (2, 1))
        context_passes(LAST, (3, 1))
        context_out(LAST - 1, WHOLE, "scalar")
        context_out(LAST, FRONT, "vector")
        context_out(LAST, (2, 1), "scalar")
        context_out(LAST, (3, 1), "vector")
